import numpy as np
import ml_dtypes


def mxq(x, axis, fmt="e4m3"):
    dtype, down = {"e4m3": (ml_dtypes.float8_e4m3fn, 7), "e5m2": (ml_dtypes.float8_e5m2, 14)}[fmt]
    v = np.moveaxis(np.asarray(x, np.float32).astype(ml_dtypes.bfloat16).astype(np.float64), axis, -1)
    blocks = v.reshape(v.shape[:-1] + (-1, 32))
    amax = np.abs(blocks).max(-1, keepdims=True)
    byte = np.maximum(np.where(amax > 0, np.frexp(amax)[1] - 1 + 127, 0) - down, 1)
    scale = np.exp2(byte - 127.0)
    codes = (blocks / scale).astype(np.float32).astype(dtype).astype(np.float64)
    return np.moveaxis((codes * scale).reshape(v.shape), -1, axis)


WIDE = False


def mx_kscale(k):
    if not WIDE:
        return np.ones(k)
    levels = np.array([20, -20, 10, -10, 0])
    a = np.random.permutation(np.resize(levels, k // 512 * 4)).reshape(k // 512, 4)
    idx = np.arange(k)
    return np.exp2(a[idx // 512, idx % 128 // 32])


BF16 = ml_dtypes.bfloat16


def bf(x):
    return np.asarray(x, np.float32).astype(BF16)


def f64(x):
    return np.asarray(x).astype(np.float64)


B, HC, WC, C, F = 512, 2, 2, 512, 512


def preact(x_crop, W_r, W_i, b_r, b_i):
    sp = f64(x_crop)
    xr = sp[:, 0].transpose(1, 2, 0, 3)
    xi = sp[:, 1].transpose(1, 2, 0, 3)
    wr = f64(W_r)
    wi = f64(W_i)
    r = xr @ wr - xi @ wi + f64(b_r)
    i = xr @ wi + xi @ wr + f64(b_i)
    return np.stack([r.transpose(2, 0, 1, 3), i.transpose(2, 0, 1, 3)], axis=1)


def setup_inputs():
    u = mx_kscale(F)
    x_crop = bf(np.stack([np.random.standard_normal((B, HC, WC, C)), np.random.standard_normal((B, HC, WC, C))], axis=1))
    W_r0 = bf(np.random.standard_normal((HC, WC, C, F)) * 0.5 / np.sqrt(C))
    W_i0 = bf(np.random.standard_normal((HC, WC, C, F)) * 0.5 / np.sqrt(C))
    b_r = bf(np.random.standard_normal(F) * 0.3)
    b_i = bf(np.random.standard_normal(F) * 0.3)
    g = bf(np.random.standard_normal((B, 2, HC, WC, F)) * np.exp2(np.random.randint(-12, 1, (B, 1, HC, WC, 1))) * 8.0 * u)
    z = preact(x_crop, W_r0, W_i0, b_r, b_i)
    return {"x_crop": x_crop,
            "W_r": bf(f64(W_r0) / u),
            "W_i": bf(f64(W_i0) / u),
            "b_r": b_r,
            "b_i": b_i,
            "z": np.asarray(z, np.float32),
            "grad_out": g}


def reference(x_crop, W_r, W_i, b_r, b_i, z, grad_out):
    dz = f64(grad_out) * (f64(z) > 0.0)
    dr = mxq(dz[:, 0].transpose(1, 2, 0, 3), 3, "e5m2")
    di = mxq(dz[:, 1].transpose(1, 2, 0, 3), 3, "e5m2")
    wr = mxq(f64(W_r), 3, "e4m3").transpose(0, 1, 3, 2)
    wi = mxq(f64(W_i), 3, "e4m3").transpose(0, 1, 3, 2)
    rr = dr @ wr
    ii = di @ wi
    ri = dr @ wi
    ir = di @ wr
    gxr = rr + ii
    gxi = ir - ri
    return np.stack([gxr.transpose(2, 0, 1, 3), gxi.transpose(2, 0, 1, 3)], axis=1)

@@ -1,0 +1,208 @@
+from contextlib import ExitStack
+
+import concourse.mybir as mybir
+from concourse.masks import make_identity
+
+F32 = mybir.dt.float32
+BF16 = mybir.dt.bfloat16
+U32 = mybir.dt.uint32
+U8 = mybir.dt.uint8
+E4M3_X4 = mybir.dt.float8_e4m3fn_x4
+E5M2_X4 = mybir.dt.float8_e5m2_x4
+ALU = mybir.AluOpType
+
+P = 128
+PACK = 4
+BATCH, HEIGHT, WIDTH, CHANNELS, FEATURES = 512, 2, 2, 512, 512
+PIXELS = HEIGHT * WIDTH
+BATCH_TILES = BATCH // P
+STEPS = BATCH_TILES * HEIGHT
+PANEL_BLOCKS = 4
+PANEL_ROWS = PANEL_BLOCKS * P
+PAIRS = FEATURES // 2
+HALVES = PAIRS // P
+ACT_BUFS = 3
+
+FLOPS = 2 * 4 * PIXELS * BATCH * CHANNELS * FEATURES
+BYTES = 2 * (2 * PIXELS * CHANNELS * FEATURES + 2 * PIXELS * BATCH * FEATURES) + 4 * (
+    2 * PIXELS * BATCH * FEATURES + 2 * PIXELS * BATCH * CHANNELS
+)
+
+
+def transpose_panel(nc, psum, stage, identity, panel, rows_first):
+    pairs = panel.bitcast(F32)
+    grouped = stage.tile([P, PANEL_ROWS, PACK], BF16, align_bytes=64)
+    grouped_pairs = grouped[:].bitcast(F32)
+    for first in range(0, PANEL_BLOCKS, 2):
+        transposed = psum.tile([P, 2, HALVES, P], F32, tag="bank")
+        for i in range(2):
+            for half in range(HALVES):
+                nc.tensor.transpose(
+                    transposed[:, i, half, :],
+                    pairs[:, first + i, half * P : (half + 1) * P],
+                    identity,
+                )
+        if rows_first:
+            nc.scalar.copy(
+                out=grouped_pairs.rearrange(
+                    "q (row block) half -> q row block half", block=PANEL_BLOCKS
+                )[:, :, first : first + 2, :],
+                in_=transposed[:].rearrange("q i half row -> q row i half"),
+            )
+        else:
+            nc.scalar.copy(
+                out=grouped_pairs.rearrange(
+                    "q (block row) half -> q block row half", block=PANEL_BLOCKS
+                )[:, first : first + 2, :, :],
+                in_=transposed[:].rearrange("q i half row -> q i row half"),
+            )
+    return grouped
+
+
+def quantise(nc, grouped, codes, scales, fp8_x4):
+    nc.vector.quantize_mx(
+        out=codes[:].bitcast(fp8_x4),
+        scales=scales[:],
+        in_=grouped[:].rearrange("q column t -> q (column t)"),
+    )
+
+
+def tile_dot_pa_v_kernel(tc, x_crop, W_r, W_i, b_r, b_i, z, grad_out, out):
+    nc = tc.nc
+
+    g_rows = grad_out.rearrange("(t p) r h w f -> t p r h (w f)", p=P)
+    z_rows = z.rearrange("(t p) r h w f -> t p r h (w f)", p=P)
+    out_rows = out.rearrange("(t p) r h w c -> t p r h (w c)", p=P)
+    weight_rows = [
+        W.rearrange("h w (p block) f -> (h w) p block f", block=PANEL_BLOCKS) for W in (W_r, W_i)
+    ]
+
+    with ExitStack() as ctx:
+        ctx.enter_context(tc.manual_schedule())
+        const = ctx.enter_context(tc.tile_pool(name="const", bufs=1))
+        w_in = ctx.enter_context(tc.tile_pool(name="w_in", bufs=2 * PIXELS))
+        act_in = ctx.enter_context(tc.tile_pool(name="act_in", bufs=ACT_BUFS))
+        w_mx = ctx.enter_context(tc.tile_pool(name="w_mx", bufs=1))
+        stage = ctx.enter_context(tc.tile_pool(name="stage", bufs=3))
+        results = ctx.enter_context(tc.tile_pool(name="results", bufs=6))
+        psum = ctx.enter_context(tc.psum_pool(name="psum", bufs=8))
+
+        identity = const.tile([P, P], F32)
+        make_identity(nc, identity[:])
+
+        g_tiles, z_tiles, w_tiles = [], [], []
+
+        def new_batch_tile():
+            g_tiles.append(act_in.tile([P, 2, HEIGHT, WIDTH * FEATURES], BF16, name="g_t"))
+            z_tiles.append(act_in.tile([P, 2, HEIGHT, WIDTH * FEATURES], F32, name="z_t"))
+
+        def load_image_rows(t, first, count):
+            rows = slice(first, first + count)
+            nc.sync.dma_start(out=g_tiles[t][:, :, rows, :], in_=g_rows[t, :, :, rows, :])
+            nc.sync.dma_start(out=z_tiles[t][:, :, rows, :], in_=z_rows[t, :, :, rows, :])
+
+        def load_batch_tile(t):
+            new_batch_tile()
+            load_image_rows(t, 0, HEIGHT)
+
+        def load_weights(h):
+            for unit in range(2 * WIDTH * h, 2 * WIDTH * (h + 1)):
+                w_t = w_in.tile([P, PANEL_BLOCKS, FEATURES], BF16, name="w_t")
+                nc.sync.dma_start(out=w_t[:], in_=weight_rows[unit % 2][unit // 2, :, :, :])
+                w_tiles.append(w_t)
+
+        new_batch_tile()
+        for h in range(HEIGHT):
+            load_image_rows(0, h, 1)
+            load_weights(h)
+        for t in range(1, ACT_BUFS):
+            load_batch_tile(t)
+
+        dz_tiles, d_codes, d_scales = [], [], []
+
+        def mask(step):
+            t, h = divmod(step, HEIGHT)
+            dz = stage.tile([P, PANEL_BLOCKS, FEATURES], BF16, name="dz")
+            nc.vector.scalar_tensor_tensor(
+                out=dz[:].rearrange("p (r w) f -> p r (w f)", r=2),
+                in0=z_tiles[t][:, :, h, :],
+                scalar=0.0,
+                in1=g_tiles[t][:, :, h, :],
+                op0=ALU.is_gt,
+                op1=ALU.mult,
+            )
+            dz_tiles.append(dz)
+            if h == HEIGHT - 1 and t + ACT_BUFS < BATCH_TILES:
+                load_batch_tile(t + ACT_BUFS)
+
+        def quantise_dz(step):
+            grouped = transpose_panel(nc, psum, stage, identity[:], dz_tiles[step][:], False)
+            codes = stage.tile([P, PANEL_ROWS], U32, name="d_codes", align_bytes=64)
+            scales = stage.tile([P, PANEL_ROWS], U8, name="d_scales", align_bytes=64)
+            quantise(nc, grouped, codes, scales, E5M2_X4)
+            d_codes.append(codes)
+            d_scales.append(scales)
+
+        w_codes, w_scales = [], []
+
+        def quantise_weights(h):
+            for unit in range(2 * WIDTH * h, 2 * WIDTH * (h + 1)):
+                grouped = transpose_panel(nc, psum, stage, identity[:], w_tiles[unit][:], True)
+                codes = w_mx.tile([P, PANEL_ROWS], U32, name="w_codes_%d" % unit, align_bytes=64)
+                scales = w_mx.tile([P, PANEL_ROWS], U8, name="w_scales_%d" % unit, align_bytes=64)
+                quantise(nc, grouped, codes, scales, E4M3_X4)
+                w_codes.append(codes)
+                w_scales.append(scales)
+
+        def multiply_and_store(step):
+            t, h = divmod(step, HEIGHT)
+            result = results.tile([P, 2, WIDTH, CHANNELS], F32, name="result")
+            for w in range(WIDTH):
+                pixel = h * WIDTH + w
+                dr_cols = slice(w * P, (w + 1) * P)
+                di_cols = slice((WIDTH + w) * P, (WIDTH + w + 1) * P)
+
+                def product(acc, d_cols, part, start, stop):
+                    nc.tensor.matmul_mx(
+                        out=acc[:],
+                        lhsT=d_codes[step][:, d_cols].bitcast(E5M2_X4),
+                        lhsT_scale=d_scales[step][:, d_cols],
+                        rhs=w_codes[2 * pixel + part][:].bitcast(E4M3_X4),
+                        rhs_scale=w_scales[2 * pixel + part][:],
+                        start=start,
+                        stop=stop,
+                    )
+
+                dr_wi = psum.tile([P, CHANNELS], F32, name="dr_wi", tag="bank")
+                real = psum.tile([P, CHANNELS], F32, name="real", tag="bank")
+                di_wr = psum.tile([P, CHANNELS], F32, name="di_wr", tag="bank")
+                product(dr_wi, dr_cols, 1, True, True)
+                product(real, dr_cols, 0, True, False)
+                product(real, di_cols, 1, False, True)
+                product(di_wr, di_cols, 0, True, True)
+
+                subtrahend = stage.tile([P, CHANNELS], F32, name="subtrahend")
+                nc.scalar.copy(out=subtrahend[:], in_=dr_wi[:])
+                nc.scalar.copy(out=result[:, 0, w, :], in_=real[:])
+                nc.vector.tensor_tensor(
+                    out=result[:, 1, w, :], in0=di_wr[:], in1=subtrahend[:], op=ALU.subtract
+                )
+            nc.sync.dma_start(
+                out=out_rows[t, :, :, h, :], in_=result[:].rearrange("p r w c -> p r (w c)")
+            )
+
+        mask(0)
+        quantise_weights(0)
+        quantise_dz(0)
+        mask(1)
+        multiply_and_store(0)
+        quantise_weights(1)
+        quantise_dz(1)
+        mask(2)
+
+        for step in range(1, STEPS):
+            if step + 2 < STEPS:
+                mask(step + 2)
+            if step + 1 < STEPS:
+                quantise_dz(step + 1)
+            multiply_and_store(step)

@@ -16,12 +16,12 @@ PACK = 4
 BATCH, HEIGHT, WIDTH, CHANNELS, FEATURES = 512, 2, 2, 512, 512
 PIXELS = HEIGHT * WIDTH
 BATCH_TILES = BATCH // P
-STEPS = BATCH_TILES * HEIGHT
+STEPS = [(t, h) for h in range(HEIGHT) for t in range(BATCH_TILES)]
 PANEL_BLOCKS = 4
 PANEL_ROWS = PANEL_BLOCKS * P
 PAIRS = FEATURES // 2
 HALVES = PAIRS // P
-ACT_BUFS = 3
+F32_BUFS = 12
 
 FLOPS = 2 * 4 * PIXELS * BATCH * CHANNELS * FEATURES
 BYTES = 2 * (2 * PIXELS * CHANNELS * FEATURES + 2 * PIXELS * BATCH * FEATURES) + 4 * (
@@ -81,10 +81,10 @@ def tile_dot_pa_v_kernel(tc, x_crop, W_r, W_i, b_r, b_i, z, grad_out, out):
         ctx.enter_context(tc.manual_schedule())
         const = ctx.enter_context(tc.tile_pool(name="const", bufs=1))
         w_in = ctx.enter_context(tc.tile_pool(name="w_in", bufs=2 * PIXELS))
-        act_in = ctx.enter_context(tc.tile_pool(name="act_in", bufs=ACT_BUFS))
+        g_in = ctx.enter_context(tc.tile_pool(name="g_in", bufs=len(STEPS)))
+        f32_ring = ctx.enter_context(tc.tile_pool(name="f32_ring", bufs=F32_BUFS))
         w_mx = ctx.enter_context(tc.tile_pool(name="w_mx", bufs=1))
         stage = ctx.enter_context(tc.tile_pool(name="stage", bufs=3))
-        results = ctx.enter_context(tc.tile_pool(name="results", bufs=6))
         psum = ctx.enter_context(tc.psum_pool(name="psum", bufs=8))
 
         identity = const.tile([P, P], F32)
@@ -92,18 +92,14 @@ def tile_dot_pa_v_kernel(tc, x_crop, W_r, W_i, b_r, b_i, z, grad_out, out):
 
         g_tiles, z_tiles, w_tiles = [], [], []
 
-        def new_batch_tile():
-            g_tiles.append(act_in.tile([P, 2, HEIGHT, WIDTH * FEATURES], BF16, name="g_t"))
-            z_tiles.append(act_in.tile([P, 2, HEIGHT, WIDTH * FEATURES], F32, name="z_t"))
-
-        def load_image_rows(t, first, count):
-            rows = slice(first, first + count)
-            nc.sync.dma_start(out=g_tiles[t][:, :, rows, :], in_=g_rows[t, :, :, rows, :])
-            nc.sync.dma_start(out=z_tiles[t][:, :, rows, :], in_=z_rows[t, :, :, rows, :])
-
-        def load_batch_tile(t):
-            new_batch_tile()
-            load_image_rows(t, 0, HEIGHT)
+        def load_step(step):
+            t, h = STEPS[step]
+            g_t = g_in.tile([P, 2, WIDTH * FEATURES], BF16, name="g_t")
+            z_t = f32_ring.tile([P, 2, WIDTH * FEATURES], F32, name="z_t", tag="f32")
+            nc.sync.dma_start(out=g_t[:], in_=g_rows[t, :, :, h, :])
+            nc.sync.dma_start(out=z_t[:], in_=z_rows[t, :, :, h, :])
+            g_tiles.append(g_t)
+            z_tiles.append(z_t)
 
         def load_weights(h):
             for unit in range(2 * WIDTH * h, 2 * WIDTH * (h + 1)):
@@ -111,29 +107,24 @@ def tile_dot_pa_v_kernel(tc, x_crop, W_r, W_i, b_r, b_i, z, grad_out, out):
                 nc.sync.dma_start(out=w_t[:], in_=weight_rows[unit % 2][unit // 2, :, :, :])
                 w_tiles.append(w_t)
 
-        new_batch_tile()
-        for h in range(HEIGHT):
-            load_image_rows(0, h, 1)
-            load_weights(h)
-        for t in range(1, ACT_BUFS):
-            load_batch_tile(t)
+        for step, (t, h) in enumerate(STEPS):
+            load_step(step)
+            if t == 0:
+                load_weights(h)
 
         dz_tiles, d_codes, d_scales = [], [], []
 
         def mask(step):
-            t, h = divmod(step, HEIGHT)
             dz = stage.tile([P, PANEL_BLOCKS, FEATURES], BF16, name="dz")
             nc.vector.scalar_tensor_tensor(
                 out=dz[:].rearrange("p (r w) f -> p r (w f)", r=2),
-                in0=z_tiles[t][:, :, h, :],
+                in0=z_tiles[step][:],
                 scalar=0.0,
-                in1=g_tiles[t][:, :, h, :],
+                in1=g_tiles[step][:],
                 op0=ALU.is_gt,
                 op1=ALU.mult,
             )
             dz_tiles.append(dz)
-            if h == HEIGHT - 1 and t + ACT_BUFS < BATCH_TILES:
-                load_batch_tile(t + ACT_BUFS)
 
         def quantise_dz(step):
             grouped = transpose_panel(nc, psum, stage, identity[:], dz_tiles[step][:], False)
@@ -145,8 +136,8 @@ def tile_dot_pa_v_kernel(tc, x_crop, W_r, W_i, b_r, b_i, z, grad_out, out):
 
         w_codes, w_scales = [], []
 
-        def quantise_weights(h):
-            for unit in range(2 * WIDTH * h, 2 * WIDTH * (h + 1)):
+        def quantise_weights(units):
+            for unit in units:
                 grouped = transpose_panel(nc, psum, stage, identity[:], w_tiles[unit][:], True)
                 codes = w_mx.tile([P, PANEL_ROWS], U32, name="w_codes_%d" % unit, align_bytes=64)
                 scales = w_mx.tile([P, PANEL_ROWS], U8, name="w_scales_%d" % unit, align_bytes=64)
@@ -155,8 +146,8 @@ def tile_dot_pa_v_kernel(tc, x_crop, W_r, W_i, b_r, b_i, z, grad_out, out):
                 w_scales.append(scales)
 
         def multiply_and_store(step):
-            t, h = divmod(step, HEIGHT)
-            result = results.tile([P, 2, WIDTH, CHANNELS], F32, name="result")
+            t, h = STEPS[step]
+            result = f32_ring.tile([P, 2, WIDTH, CHANNELS], F32, name="result", tag="f32")
             for w in range(WIDTH):
                 pixel = h * WIDTH + w
                 dr_cols = slice(w * P, (w + 1) * P)
@@ -192,17 +183,17 @@ def tile_dot_pa_v_kernel(tc, x_crop, W_r, W_i, b_r, b_i, z, grad_out, out):
             )
 
         mask(0)
-        quantise_weights(0)
+        quantise_weights(range(0, 4))
         quantise_dz(0)
         mask(1)
-        multiply_and_store(0)
-        quantise_weights(1)
-        quantise_dz(1)
-        mask(2)
 
-        for step in range(1, STEPS):
-            if step + 2 < STEPS:
+        for step in range(len(STEPS)):
+            if step + 2 < len(STEPS):
                 mask(step + 2)
-            if step + 1 < STEPS:
+            if step + 1 < len(STEPS):
                 quantise_dz(step + 1)
+            if step == 2:
+                quantise_weights(range(4, 6))
+            if step == 3:
+                quantise_weights(range(6, 8))
             multiply_and_store(step)

@@ -16,12 +16,12 @@ PACK = 4
 BATCH, HEIGHT, WIDTH, CHANNELS, FEATURES = 512, 2, 2, 512, 512
 PIXELS = HEIGHT * WIDTH
 BATCH_TILES = BATCH // P
-STEPS = [(t, h) for h in range(HEIGHT) for t in range(BATCH_TILES)]
-PANEL_BLOCKS = 4
-PANEL_ROWS = PANEL_BLOCKS * P
+STEPS = BATCH_TILES * HEIGHT
+D_BLOCKS = 4
+W_BLOCKS = 8
 PAIRS = FEATURES // 2
 HALVES = PAIRS // P
-F32_BUFS = 12
+F32_BUFS = 6
 
 FLOPS = 2 * 4 * PIXELS * BATCH * CHANNELS * FEATURES
 BYTES = 2 * (2 * PIXELS * CHANNELS * FEATURES + 2 * PIXELS * BATCH * FEATURES) + 4 * (
@@ -30,10 +30,13 @@ BYTES = 2 * (2 * PIXELS * CHANNELS * FEATURES + 2 * PIXELS * BATCH * FEATURES) +
 
 
 def transpose_panel(nc, psum, stage, identity, panel, rows_first):
+    blocks = panel.shape[1]
     pairs = panel.bitcast(F32)
-    grouped = stage.tile([P, PANEL_ROWS, PACK], BF16, align_bytes=64)
+    grouped = stage.tile(
+        [P, blocks * P, PACK], BF16, name="w_grouped" if rows_first else "d_grouped", align_bytes=64
+    )
     grouped_pairs = grouped[:].bitcast(F32)
-    for first in range(0, PANEL_BLOCKS, 2):
+    for first in range(0, blocks, 2):
         transposed = psum.tile([P, 2, HALVES, P], F32, tag="bank")
         for i in range(2):
             for half in range(HALVES):
@@ -45,14 +48,14 @@ def transpose_panel(nc, psum, stage, identity, panel, rows_first):
         if rows_first:
             nc.scalar.copy(
                 out=grouped_pairs.rearrange(
-                    "q (row block) half -> q row block half", block=PANEL_BLOCKS
+                    "q (row block) half -> q row block half", block=blocks
                 )[:, :, first : first + 2, :],
                 in_=transposed[:].rearrange("q i half row -> q row i half"),
             )
         else:
             nc.scalar.copy(
                 out=grouped_pairs.rearrange(
-                    "q (block row) half -> q block row half", block=PANEL_BLOCKS
+                    "q (block row) half -> q block row half", block=blocks
                 )[:, first : first + 2, :, :],
                 in_=transposed[:].rearrange("q i half row -> q i row half"),
             )
@@ -74,16 +77,18 @@ def tile_dot_pa_v_kernel(tc, x_crop, W_r, W_i, b_r, b_i, z, grad_out, out):
     z_rows = z.rearrange("(t p) r h w f -> t p r h (w f)", p=P)
     out_rows = out.rearrange("(t p) r h w c -> t p r h (w c)", p=P)
     weight_rows = [
-        W.rearrange("h w (p block) f -> (h w) p block f", block=PANEL_BLOCKS) for W in (W_r, W_i)
+        W.rearrange("h w c f -> h (w c) f").rearrange("h (p block) f -> h p block f", block=W_BLOCKS)
+        for W in (W_r, W_i)
     ]
 
     with ExitStack() as ctx:
         ctx.enter_context(tc.manual_schedule())
         const = ctx.enter_context(tc.tile_pool(name="const", bufs=1))
-        w_in = ctx.enter_context(tc.tile_pool(name="w_in", bufs=2 * PIXELS))
-        g_in = ctx.enter_context(tc.tile_pool(name="g_in", bufs=len(STEPS)))
+        w_in = ctx.enter_context(tc.tile_pool(name="w_in", bufs=2 * HEIGHT))
+        g_in = ctx.enter_context(tc.tile_pool(name="g_in", bufs=BATCH_TILES))
         f32_ring = ctx.enter_context(tc.tile_pool(name="f32_ring", bufs=F32_BUFS))
         w_mx = ctx.enter_context(tc.tile_pool(name="w_mx", bufs=1))
+        w_stage = ctx.enter_context(tc.tile_pool(name="w_stage", bufs=2))
         stage = ctx.enter_context(tc.tile_pool(name="stage", bufs=3))
         psum = ctx.enter_context(tc.psum_pool(name="psum", bufs=8))
 
@@ -92,35 +97,39 @@ def tile_dot_pa_v_kernel(tc, x_crop, W_r, W_i, b_r, b_i, z, grad_out, out):
 
         g_tiles, z_tiles, w_tiles = [], [], []
 
-        def load_step(step):
-            t, h = STEPS[step]
-            g_t = g_in.tile([P, 2, WIDTH * FEATURES], BF16, name="g_t")
-            z_t = f32_ring.tile([P, 2, WIDTH * FEATURES], F32, name="z_t", tag="f32")
-            nc.sync.dma_start(out=g_t[:], in_=g_rows[t, :, :, h, :])
-            nc.sync.dma_start(out=z_t[:], in_=z_rows[t, :, :, h, :])
+        def load_batch_tile(t, z_pieces):
+            g_t = g_in.tile([P, 2, HEIGHT, WIDTH * FEATURES], BF16, name="g_t")
+            z_t = f32_ring.tile([P, 2, HEIGHT, WIDTH * FEATURES], F32, name="z_t", tag="f32")
+            nc.sync.dma_start(out=g_t[:], in_=g_rows[t, :, :, :, :])
+            count = HEIGHT // z_pieces
+            for first in range(0, HEIGHT, count):
+                rows = slice(first, first + count)
+                nc.sync.dma_start(out=z_t[:, :, rows, :], in_=z_rows[t, :, :, rows, :])
             g_tiles.append(g_t)
             z_tiles.append(z_t)
 
         def load_weights(h):
-            for unit in range(2 * WIDTH * h, 2 * WIDTH * (h + 1)):
-                w_t = w_in.tile([P, PANEL_BLOCKS, FEATURES], BF16, name="w_t")
-                nc.sync.dma_start(out=w_t[:], in_=weight_rows[unit % 2][unit // 2, :, :, :])
+            for part in range(2):
+                w_t = w_in.tile([P, W_BLOCKS, FEATURES], BF16, name="w_t")
+                nc.sync.dma_start(out=w_t[:], in_=weight_rows[part][h, :, :, :])
                 w_tiles.append(w_t)
 
-        for step, (t, h) in enumerate(STEPS):
-            load_step(step)
-            if t == 0:
-                load_weights(h)
+        load_weights(0)
+        load_batch_tile(0, HEIGHT)
+        load_weights(1)
+        for t in range(1, BATCH_TILES):
+            load_batch_tile(t, 1)
 
         dz_tiles, d_codes, d_scales = [], [], []
 
         def mask(step):
-            dz = stage.tile([P, PANEL_BLOCKS, FEATURES], BF16, name="dz")
+            t, h = divmod(step, HEIGHT)
+            dz = stage.tile([P, D_BLOCKS, FEATURES], BF16, name="dz")
             nc.vector.scalar_tensor_tensor(
                 out=dz[:].rearrange("p (r w) f -> p r (w f)", r=2),
-                in0=z_tiles[step][:],
+                in0=z_tiles[t][:, :, h, :],
                 scalar=0.0,
-                in1=g_tiles[step][:],
+                in1=g_tiles[t][:, :, h, :],
                 op0=ALU.is_gt,
                 op1=ALU.mult,
             )
@@ -128,28 +137,36 @@ def tile_dot_pa_v_kernel(tc, x_crop, W_r, W_i, b_r, b_i, z, grad_out, out):
 
         def quantise_dz(step):
             grouped = transpose_panel(nc, psum, stage, identity[:], dz_tiles[step][:], False)
-            codes = stage.tile([P, PANEL_ROWS], U32, name="d_codes", align_bytes=64)
-            scales = stage.tile([P, PANEL_ROWS], U8, name="d_scales", align_bytes=64)
+            codes = stage.tile([P, D_BLOCKS * P], U32, name="d_codes", align_bytes=64)
+            scales = stage.tile([P, D_BLOCKS * P], U8, name="d_scales", align_bytes=64)
             quantise(nc, grouped, codes, scales, E5M2_X4)
             d_codes.append(codes)
             d_scales.append(scales)
 
         w_codes, w_scales = [], []
 
-        def quantise_weights(units):
-            for unit in units:
-                grouped = transpose_panel(nc, psum, stage, identity[:], w_tiles[unit][:], True)
-                codes = w_mx.tile([P, PANEL_ROWS], U32, name="w_codes_%d" % unit, align_bytes=64)
-                scales = w_mx.tile([P, PANEL_ROWS], U8, name="w_scales_%d" % unit, align_bytes=64)
-                quantise(nc, grouped, codes, scales, E4M3_X4)
-                w_codes.append(codes)
-                w_scales.append(scales)
+        def quantise_weights(h, part):
+            grouped = transpose_panel(
+                nc, psum, w_stage, identity[:], w_tiles[2 * h + part][:], True
+            )
+            codes = w_mx.tile([P, W_BLOCKS * P], U32, name="w_codes_%d%d" % (h, part), align_bytes=64)
+            scales = w_mx.tile([P, W_BLOCKS * P], U8, name="w_scales_%d%d" % (h, part), align_bytes=64)
+            quantise(nc, grouped, codes, scales, E4M3_X4)
+            w_codes.append(codes)
+            w_scales.append(scales)
+
+        results = []
 
         def multiply_and_store(step):
-            t, h = STEPS[step]
-            result = f32_ring.tile([P, 2, WIDTH, CHANNELS], F32, name="result", tag="f32")
+            t, h = divmod(step, HEIGHT)
+            if h == 0:
+                new_result = f32_ring.tile(
+                    [P, 2, HEIGHT, WIDTH * CHANNELS], F32, name="result", tag="f32"
+                )
+                results.append(new_result)
+            result = results[t]
             for w in range(WIDTH):
-                pixel = h * WIDTH + w
+                c_cols = slice(w * CHANNELS, (w + 1) * CHANNELS)
                 dr_cols = slice(w * P, (w + 1) * P)
                 di_cols = slice((WIDTH + w) * P, (WIDTH + w + 1) * P)
 
@@ -158,8 +175,8 @@ def tile_dot_pa_v_kernel(tc, x_crop, W_r, W_i, b_r, b_i, z, grad_out, out):
                         out=acc[:],
                         lhsT=d_codes[step][:, d_cols].bitcast(E5M2_X4),
                         lhsT_scale=d_scales[step][:, d_cols],
-                        rhs=w_codes[2 * pixel + part][:].bitcast(E4M3_X4),
-                        rhs_scale=w_scales[2 * pixel + part][:],
+                        rhs=w_codes[2 * h + part][:, c_cols].bitcast(E4M3_X4),
+                        rhs_scale=w_scales[2 * h + part][:, c_cols],
                         start=start,
                         stop=stop,
                     )
@@ -174,26 +191,32 @@ def tile_dot_pa_v_kernel(tc, x_crop, W_r, W_i, b_r, b_i, z, grad_out, out):
 
                 subtrahend = stage.tile([P, CHANNELS], F32, name="subtrahend")
                 nc.scalar.copy(out=subtrahend[:], in_=dr_wi[:])
-                nc.scalar.copy(out=result[:, 0, w, :], in_=real[:])
+                nc.scalar.copy(out=result[:, 0, h, c_cols], in_=real[:])
                 nc.vector.tensor_tensor(
-                    out=result[:, 1, w, :], in0=di_wr[:], in1=subtrahend[:], op=ALU.subtract
+                    out=result[:, 1, h, c_cols], in0=di_wr[:], in1=subtrahend[:], op=ALU.subtract
                 )
-            nc.sync.dma_start(
-                out=out_rows[t, :, :, h, :], in_=result[:].rearrange("p r w c -> p r (w c)")
-            )
+            if t >= BATCH_TILES // 2:
+                rows = slice(h, h + 1)
+            elif h == HEIGHT - 1:
+                rows = slice(0, HEIGHT)
+            else:
+                return
+            nc.sync.dma_start(out=out_rows[t, :, :, rows, :], in_=result[:, :, rows, :])
 
+        quantise_weights(0, 0)
+        quantise_weights(0, 1)
         mask(0)
-        quantise_weights(range(0, 4))
         quantise_dz(0)
         mask(1)
+        quantise_weights(1, 0)
+        quantise_dz(1)
+        quantise_weights(1, 1)
+        multiply_and_store(0)
+        mask(2)
 
-        for step in range(len(STEPS)):
-            if step + 2 < len(STEPS):
+        for step in range(1, STEPS):
+            if step + 2 < STEPS:
                 mask(step + 2)
-            if step + 1 < len(STEPS):
+            if step + 1 < STEPS:
                 quantise_dz(step + 1)
-            if step == 2:
-                quantise_weights(range(4, 6))
-            if step == 3:
-                quantise_weights(range(6, 8))
             multiply_and_store(step)

@@ -16,7 +16,10 @@ PACK = 4
 BATCH, HEIGHT, WIDTH, CHANNELS, FEATURES = 512, 2, 2, 512, 512
 PIXELS = HEIGHT * WIDTH
 BATCH_TILES = BATCH // P
-STEPS = BATCH_TILES * HEIGHT
+PAIRED_TILES = 2
+STEPS = [(t, h) for h in range(HEIGHT) for t in range(PAIRED_TILES)] + [
+    (t, h) for t in range(PAIRED_TILES, BATCH_TILES) for h in range(HEIGHT)
+]
 D_BLOCKS = 4
 W_BLOCKS = 8
 PAIRS = FEATURES // 2
@@ -97,16 +100,16 @@ def tile_dot_pa_v_kernel(tc, x_crop, W_r, W_i, b_r, b_i, z, grad_out, out):
 
         g_tiles, z_tiles, w_tiles = [], [], []
 
-        def load_batch_tile(t, z_pieces):
+        def load_g(t):
             g_t = g_in.tile([P, 2, HEIGHT, WIDTH * FEATURES], BF16, name="g_t")
-            z_t = f32_ring.tile([P, 2, HEIGHT, WIDTH * FEATURES], F32, name="z_t", tag="f32")
             nc.sync.dma_start(out=g_t[:], in_=g_rows[t, :, :, :, :])
-            count = HEIGHT // z_pieces
-            for first in range(0, HEIGHT, count):
-                rows = slice(first, first + count)
-                nc.sync.dma_start(out=z_t[:, :, rows, :], in_=z_rows[t, :, :, rows, :])
             g_tiles.append(g_t)
-            z_tiles.append(z_t)
+
+        def load_z(t, rows):
+            if len(z_tiles) == t:
+                z_t = f32_ring.tile([P, 2, HEIGHT, WIDTH * FEATURES], F32, name="z_t", tag="f32")
+                z_tiles.append(z_t)
+            nc.sync.dma_start(out=z_tiles[t][:, :, rows, :], in_=z_rows[t, :, :, rows, :])
 
         def load_weights(h):
             for part in range(2):
@@ -114,16 +117,22 @@ def tile_dot_pa_v_kernel(tc, x_crop, W_r, W_i, b_r, b_i, z, grad_out, out):
                 nc.sync.dma_start(out=w_t[:], in_=weight_rows[part][h, :, :, :])
                 w_tiles.append(w_t)
 
+        load_g(0)
+        load_z(0, slice(0, 1))
         load_weights(0)
-        load_batch_tile(0, HEIGHT)
+        load_g(1)
+        load_z(1, slice(0, 1))
+        for t in range(PAIRED_TILES):
+            load_z(t, slice(1, 2))
         load_weights(1)
-        for t in range(1, BATCH_TILES):
-            load_batch_tile(t, 1)
+        for t in range(PAIRED_TILES, BATCH_TILES):
+            load_g(t)
+            load_z(t, slice(0, HEIGHT))
 
-        dz_tiles, d_codes, d_scales = [], [], []
+        dz_tiles, d_grouped, d_codes, d_scales = [], [], [], []
 
         def mask(step):
-            t, h = divmod(step, HEIGHT)
+            t, h = STEPS[step]
             dz = stage.tile([P, D_BLOCKS, FEATURES], BF16, name="dz")
             nc.vector.scalar_tensor_tensor(
                 out=dz[:].rearrange("p (r w) f -> p r (w f)", r=2),
@@ -135,30 +144,39 @@ def tile_dot_pa_v_kernel(tc, x_crop, W_r, W_i, b_r, b_i, z, grad_out, out):
             )
             dz_tiles.append(dz)
 
+        def transpose_dz(step):
+            d_grouped.append(
+                transpose_panel(nc, psum, stage, identity[:], dz_tiles[step][:], False)
+            )
+
         def quantise_dz(step):
-            grouped = transpose_panel(nc, psum, stage, identity[:], dz_tiles[step][:], False)
             codes = stage.tile([P, D_BLOCKS * P], U32, name="d_codes", align_bytes=64)
             scales = stage.tile([P, D_BLOCKS * P], U8, name="d_scales", align_bytes=64)
-            quantise(nc, grouped, codes, scales, E5M2_X4)
+            quantise(nc, d_grouped[step], codes, scales, E5M2_X4)
             d_codes.append(codes)
             d_scales.append(scales)
 
         w_codes, w_scales = [], []
 
-        def quantise_weights(h, part):
-            grouped = transpose_panel(
+        def transpose_weights(h, part):
+            return transpose_panel(
                 nc, psum, w_stage, identity[:], w_tiles[2 * h + part][:], True
             )
+
+        def quantise_grouped_weights(grouped, h, part):
             codes = w_mx.tile([P, W_BLOCKS * P], U32, name="w_codes_%d%d" % (h, part), align_bytes=64)
             scales = w_mx.tile([P, W_BLOCKS * P], U8, name="w_scales_%d%d" % (h, part), align_bytes=64)
             quantise(nc, grouped, codes, scales, E4M3_X4)
             w_codes.append(codes)
             w_scales.append(scales)
 
+        def quantise_weights(h, part):
+            quantise_grouped_weights(transpose_weights(h, part), h, part)
+
         results = []
 
         def multiply_and_store(step):
-            t, h = divmod(step, HEIGHT)
+            t, h = STEPS[step]
             if h == 0:
                 new_result = f32_ring.tile(
                     [P, 2, HEIGHT, WIDTH * CHANNELS], F32, name="result", tag="f32"
@@ -203,20 +221,22 @@ def tile_dot_pa_v_kernel(tc, x_crop, W_r, W_i, b_r, b_i, z, grad_out, out):
                 return
             nc.sync.dma_start(out=out_rows[t, :, :, rows, :], in_=result[:, :, rows, :])
 
-        quantise_weights(0, 0)
-        quantise_weights(0, 1)
         mask(0)
+        quantise_weights(0, 0)
+        transpose_dz(0)
+        w_grouped = transpose_weights(0, 1)
         quantise_dz(0)
         mask(1)
-        quantise_weights(1, 0)
-        quantise_dz(1)
-        quantise_weights(1, 1)
-        multiply_and_store(0)
-        mask(2)
+        quantise_grouped_weights(w_grouped, 0, 1)
 
-        for step in range(1, STEPS):
-            if step + 2 < STEPS:
+        for step in range(len(STEPS)):
+            if step + 1 < len(STEPS):
+                transpose_dz(step + 1)
+            if step + 2 < len(STEPS):
                 mask(step + 2)
-            if step + 1 < STEPS:
+            if step + 1 < len(STEPS):
                 quantise_dz(step + 1)
+            if step == PAIRED_TILES - 1:
+                quantise_weights(1, 0)
+                quantise_weights(1, 1)
             multiply_and_store(step)

@@ -213,6 +213,18 @@ def tile_dot_pa_v_kernel(tc, x_crop, W_r, W_i, b_r, b_i, z, grad_out, out):
                 nc.vector.tensor_tensor(
                     out=result[:, 1, h, c_cols], in0=di_wr[:], in1=subtrahend[:], op=ALU.subtract
                 )
+                if step == len(STEPS) - 1:
+                    pieces = (slice(0, 1), slice(1, 2))
+                elif t == BATCH_TILES - 1:
+                    pieces = (slice(0, 2),)
+                else:
+                    pieces = ()
+                for parts in pieces:
+                    nc.sync.dma_start(
+                        out=out_rows[t, :, parts, h, c_cols], in_=result[:, parts, h, c_cols]
+                    )
+            if t == BATCH_TILES - 1:
+                return
             if t >= BATCH_TILES // 2:
                 rows = slice(h, h + 1)
             elif h == HEIGHT - 1:

from contextlib import ExitStack

import concourse.mybir as mybir
from concourse.masks import make_identity

F32 = mybir.dt.float32
BF16 = mybir.dt.bfloat16
U32 = mybir.dt.uint32
U8 = mybir.dt.uint8
E4M3_X4 = mybir.dt.float8_e4m3fn_x4
E5M2_X4 = mybir.dt.float8_e5m2_x4
ALU = mybir.AluOpType

P = 128
PACK = 4
BATCH, HEIGHT, WIDTH, CHANNELS, FEATURES = 512, 2, 2, 512, 512
PIXELS = HEIGHT * WIDTH
BATCH_TILES = BATCH // P
PAIRED_TILES = 2
STEPS = [(t, h) for h in range(HEIGHT) for t in range(PAIRED_TILES)] + [
    (t, h) for t in range(PAIRED_TILES, BATCH_TILES) for h in range(HEIGHT)
]
D_BLOCKS = 4
W_BLOCKS = 8
PAIRS = FEATURES // 2
HALVES = PAIRS // P
F32_BUFS = 6

FLOPS = 2 * 4 * PIXELS * BATCH * CHANNELS * FEATURES
BYTES = 2 * (2 * PIXELS * CHANNELS * FEATURES + 2 * PIXELS * BATCH * FEATURES) + 4 * (
    2 * PIXELS * BATCH * FEATURES + 2 * PIXELS * BATCH * CHANNELS
)


def transpose_panel(nc, psum, stage, identity, panel, rows_first):
    blocks = panel.shape[1]
    pairs = panel.bitcast(F32)
    grouped = stage.tile(
        [P, blocks * P, PACK], BF16, name="w_grouped" if rows_first else "d_grouped", align_bytes=64
    )
    grouped_pairs = grouped[:].bitcast(F32)
    for first in range(0, blocks, 2):
        transposed = psum.tile([P, 2, HALVES, P], F32, tag="bank")
        for i in range(2):
            for half in range(HALVES):
                nc.tensor.transpose(
                    transposed[:, i, half, :],
                    pairs[:, first + i, half * P : (half + 1) * P],
                    identity,
                )
        if rows_first:
            nc.scalar.copy(
                out=grouped_pairs.rearrange(
                    "q (row block) half -> q row block half", block=blocks
                )[:, :, first : first + 2, :],
                in_=transposed[:].rearrange("q i half row -> q row i half"),
            )
        else:
            nc.scalar.copy(
                out=grouped_pairs.rearrange(
                    "q (block row) half -> q block row half", block=blocks
                )[:, first : first + 2, :, :],
                in_=transposed[:].rearrange("q i half row -> q i row half"),
            )
    return grouped


def quantise(nc, grouped, codes, scales, fp8_x4):
    nc.vector.quantize_mx(
        out=codes[:].bitcast(fp8_x4),
        scales=scales[:],
        in_=grouped[:].rearrange("q column t -> q (column t)"),
    )


def tile_dot_pa_v_kernel(tc, x_crop, W_r, W_i, b_r, b_i, z, grad_out, out):
    nc = tc.nc

    g_rows = grad_out.rearrange("(t p) r h w f -> t p r h (w f)", p=P)
    z_rows = z.rearrange("(t p) r h w f -> t p r h (w f)", p=P)
    out_rows = out.rearrange("(t p) r h w c -> t p r h (w c)", p=P)
    weight_rows = [
        W.rearrange("h w c f -> h (w c) f").rearrange("h (p block) f -> h p block f", block=W_BLOCKS)
        for W in (W_r, W_i)
    ]

    with ExitStack() as ctx:
        ctx.enter_context(tc.manual_schedule())
        const = ctx.enter_context(tc.tile_pool(name="const", bufs=1))
        w_in = ctx.enter_context(tc.tile_pool(name="w_in", bufs=2 * HEIGHT))
        g_in = ctx.enter_context(tc.tile_pool(name="g_in", bufs=BATCH_TILES))
        f32_ring = ctx.enter_context(tc.tile_pool(name="f32_ring", bufs=F32_BUFS))
        w_mx = ctx.enter_context(tc.tile_pool(name="w_mx", bufs=1))
        w_stage = ctx.enter_context(tc.tile_pool(name="w_stage", bufs=2))
        stage = ctx.enter_context(tc.tile_pool(name="stage", bufs=3))
        psum = ctx.enter_context(tc.psum_pool(name="psum", bufs=8))

        identity = const.tile([P, P], F32)
        make_identity(nc, identity[:])

        g_tiles, z_tiles, w_tiles = [], [], []

        def load_g(t):
            g_t = g_in.tile([P, 2, HEIGHT, WIDTH * FEATURES], BF16, name="g_t")
            nc.sync.dma_start(out=g_t[:], in_=g_rows[t, :, :, :, :])
            g_tiles.append(g_t)

        def load_z(t, rows):
            if len(z_tiles) == t:
                z_t = f32_ring.tile([P, 2, HEIGHT, WIDTH * FEATURES], F32, name="z_t", tag="f32")
                z_tiles.append(z_t)
            nc.sync.dma_start(out=z_tiles[t][:, :, rows, :], in_=z_rows[t, :, :, rows, :])

        def load_weights(h):
            for part in range(2):
                w_t = w_in.tile([P, W_BLOCKS, FEATURES], BF16, name="w_t")
                nc.sync.dma_start(out=w_t[:], in_=weight_rows[part][h, :, :, :])
                w_tiles.append(w_t)

        load_g(0)
        load_z(0, slice(0, 1))
        load_weights(0)
        load_g(1)
        load_z(1, slice(0, 1))
        for t in range(PAIRED_TILES):
            load_z(t, slice(1, 2))
        load_weights(1)
        for t in range(PAIRED_TILES, BATCH_TILES):
            load_g(t)
            load_z(t, slice(0, HEIGHT))

        dz_tiles, d_grouped, d_codes, d_scales = [], [], [], []

        def mask(step):
            t, h = STEPS[step]
            dz = stage.tile([P, D_BLOCKS, FEATURES], BF16, name="dz")
            nc.vector.scalar_tensor_tensor(
                out=dz[:].rearrange("p (r w) f -> p r (w f)", r=2),
                in0=z_tiles[t][:, :, h, :],
                scalar=0.0,
                in1=g_tiles[t][:, :, h, :],
                op0=ALU.is_gt,
                op1=ALU.mult,
            )
            dz_tiles.append(dz)

        def transpose_dz(step):
            d_grouped.append(
                transpose_panel(nc, psum, stage, identity[:], dz_tiles[step][:], False)
            )

        def quantise_dz(step):
            codes = stage.tile([P, D_BLOCKS * P], U32, name="d_codes", align_bytes=64)
            scales = stage.tile([P, D_BLOCKS * P], U8, name="d_scales", align_bytes=64)
            quantise(nc, d_grouped[step], codes, scales, E5M2_X4)
            d_codes.append(codes)
            d_scales.append(scales)

        w_codes, w_scales = [], []

        def transpose_weights(h, part):
            return transpose_panel(
                nc, psum, w_stage, identity[:], w_tiles[2 * h + part][:], True
            )

        def quantise_grouped_weights(grouped, h, part):
            codes = w_mx.tile([P, W_BLOCKS * P], U32, name="w_codes_%d%d" % (h, part), align_bytes=64)
            scales = w_mx.tile([P, W_BLOCKS * P], U8, name="w_scales_%d%d" % (h, part), align_bytes=64)
            quantise(nc, grouped, codes, scales, E4M3_X4)
            w_codes.append(codes)
            w_scales.append(scales)

        def quantise_weights(h, part):
            quantise_grouped_weights(transpose_weights(h, part), h, part)

        results = []

        def multiply_and_store(step):
            t, h = STEPS[step]
            if h == 0:
                new_result = f32_ring.tile(
                    [P, 2, HEIGHT, WIDTH * CHANNELS], F32, name="result", tag="f32"
                )
                results.append(new_result)
            result = results[t]
            for w in range(WIDTH):
                c_cols = slice(w * CHANNELS, (w + 1) * CHANNELS)
                dr_cols = slice(w * P, (w + 1) * P)
                di_cols = slice((WIDTH + w) * P, (WIDTH + w + 1) * P)

                def product(acc, d_cols, part, start, stop):
                    nc.tensor.matmul_mx(
                        out=acc[:],
                        lhsT=d_codes[step][:, d_cols].bitcast(E5M2_X4),
                        lhsT_scale=d_scales[step][:, d_cols],
                        rhs=w_codes[2 * h + part][:, c_cols].bitcast(E4M3_X4),
                        rhs_scale=w_scales[2 * h + part][:, c_cols],
                        start=start,
                        stop=stop,
                    )

                dr_wi = psum.tile([P, CHANNELS], F32, name="dr_wi", tag="bank")
                real = psum.tile([P, CHANNELS], F32, name="real", tag="bank")
                di_wr = psum.tile([P, CHANNELS], F32, name="di_wr", tag="bank")
                product(dr_wi, dr_cols, 1, True, True)
                product(real, dr_cols, 0, True, False)
                product(real, di_cols, 1, False, True)
                product(di_wr, di_cols, 0, True, True)

                subtrahend = stage.tile([P, CHANNELS], F32, name="subtrahend")
                nc.scalar.copy(out=subtrahend[:], in_=dr_wi[:])
                nc.scalar.copy(out=result[:, 0, h, c_cols], in_=real[:])
                nc.vector.tensor_tensor(
                    out=result[:, 1, h, c_cols], in0=di_wr[:], in1=subtrahend[:], op=ALU.subtract
                )
                if step == len(STEPS) - 1:
                    pieces = (slice(0, 1), slice(1, 2))
                elif t == BATCH_TILES - 1:
                    pieces = (slice(0, 2),)
                else:
                    pieces = ()
                for parts in pieces:
                    nc.sync.dma_start(
                        out=out_rows[t, :, parts, h, c_cols], in_=result[:, parts, h, c_cols]
                    )
            if t == BATCH_TILES - 1:
                return
            if t >= BATCH_TILES // 2:
                rows = slice(h, h + 1)
            elif h == HEIGHT - 1:
                rows = slice(0, HEIGHT)
            else:
                return
            nc.sync.dma_start(out=out_rows[t, :, :, rows, :], in_=result[:, :, rows, :])

        mask(0)
        quantise_weights(0, 0)
        transpose_dz(0)
        w_grouped = transpose_weights(0, 1)
        quantise_dz(0)
        mask(1)
        quantise_grouped_weights(w_grouped, 0, 1)

        for step in range(len(STEPS)):
            if step + 1 < len(STEPS):
                transpose_dz(step + 1)
            if step + 2 < len(STEPS):
                mask(step + 2)
            if step + 1 < len(STEPS):
                quantise_dz(step + 1)
            if step == PAIRED_TILES - 1:
                quantise_weights(1, 0)
                quantise_weights(1, 1)
            multiply_and_store(step)
